import numpy as np
import ml_dtypes


def mxq(x, axis, fmt="e4m3"):
    dtype, down = {"e4m3": (ml_dtypes.float8_e4m3fn, 7), "e5m2": (ml_dtypes.float8_e5m2, 14)}[fmt]
    v = np.moveaxis(np.asarray(x, np.float32).astype(ml_dtypes.bfloat16).astype(np.float64), axis, -1)
    blocks = v.reshape(v.shape[:-1] + (-1, 32))
    amax = np.abs(blocks).max(-1, keepdims=True)
    byte = np.maximum(np.where(amax > 0, np.frexp(amax)[1] - 1 + 127, 0) - down, 1)
    scale = np.exp2(byte - 127.0)
    codes = (blocks / scale).astype(np.float32).astype(dtype).astype(np.float64)
    return np.moveaxis((codes * scale).reshape(v.shape), -1, axis)


WIDE = False


def mx_kscale(k):
    if not WIDE:
        return np.ones(k)
    levels = np.array([10, -10, 5, -5, 0])
    if k % 512:
        return np.exp2(np.random.permutation(np.resize(levels, k // 32))).repeat(32)
    a = np.empty((k // 512, 16))
    for p in range(k // 512):
        a[p, :8] = np.random.permutation(np.resize(levels, 8))
        for g in range(8):
            far = levels[np.abs(levels - a[p, g]) >= 10]
            a[p, g + 8] = far[np.random.randint(len(far))]
    return np.exp2(a.ravel()).repeat(32)


BF16 = ml_dtypes.bfloat16


def bf(x):
    return np.asarray(x, np.float32).astype(BF16)


def f64(x):
    return np.asarray(x).astype(np.float64)


B, S, D, H, QL, KL, ND, VD, RD = 4, 256, 2048, 16, 512, 512, 128, 128, 128
BASE = 10000.0


def rope(v):
    d = v.shape[-1]
    inv_freq = BASE ** (-np.arange(0, d, 2) / d)
    ang = np.arange(v.shape[1])[:, None] * inv_freq[None, :]
    cos = np.cos(ang)[None, :, None, :]
    sin = np.sin(ang)[None, :, None, :]
    v1 = v[..., 0::2]
    v2 = v[..., 1::2]
    o1 = v1 * cos - v2 * sin
    o2 = v1 * sin + v2 * cos
    return np.stack([o1, o2], axis=-1).reshape(v.shape)


def setup_inputs():
    s, t = mx_kscale(D), mx_kscale(KL)
    tc = np.concatenate([t, np.ones(RD)])
    return {"x": bf(np.random.standard_normal((B, S, D)) * s),
            "Wkva": bf(np.random.standard_normal((D, KL + RD)) / np.sqrt(D) / s[:, None] * tc),
            "Wkvb": bf(np.random.standard_normal((KL, H * (ND + VD))) / np.sqrt(KL) / t[:, None])}


def reference(x, Wkva, Wkvb):
    ckv = mxq(f64(x), 2, "e4m3") @ mxq(f64(Wkva), 0, "e4m3")
    compressed_kv, k_pe = ckv[..., :KL], ckv[..., KL:]
    k_pe = np.broadcast_to(k_pe[:, :, None, :], (B, S, H, RD))
    kv = (mxq(compressed_kv, 2, "e4m3") @ mxq(f64(Wkvb), 0, "e4m3")).reshape(B, S, H, ND + VD)
    k_nope, v = kv[..., :ND], kv[..., ND:]
    kf = np.concatenate([k_nope, rope(k_pe)], axis=-1)
    return kf, v

@@ -1,0 +1,278 @@
+import math
+from contextlib import ExitStack
+
+import concourse.mybir as mybir
+from concourse.masks import make_identity
+
+BF16 = mybir.dt.bfloat16
+F32 = mybir.dt.float32
+U32 = mybir.dt.uint32
+U8 = mybir.dt.uint8
+FP8X4 = mybir.dt.float8_e4m3fn_x4
+ALU = mybir.AluOpType
+
+P = 128
+PACK = 4
+K_PASS = P * PACK
+BANK = 512
+
+TOKENS = 4 * 256
+POSITIONS = 256
+D_MODEL = 2048
+HEADS = 16
+LATENT = 512
+ROPE = 128
+NOPE = 128
+VDIM = 128
+ROPE_BASE = 10000.0
+
+TOKEN_TILES = TOKENS // P
+X_PASSES = D_MODEL // K_PASS
+PAIRS = ROPE // 2
+HEAD_GROUP = BANK // NOPE
+HEAD_GROUPS = HEADS // HEAD_GROUP
+UNIT = BANK * PACK
+RUN = 4
+WB_PIECES = 2
+ROUND_MAGIC = 1.5 * 2.0**23
+
+FLOPS = 2 * TOKENS * D_MODEL * (LATENT + ROPE) + 2 * TOKENS * LATENT * HEADS * (NOPE + VDIM)
+
+
+def span(index, width):
+    return slice(index * width, (index + 1) * width)
+
+
+def tile_multilatentattention_pb_kernel(tc, x, Wkva, Wkvb, out_0, out_1):
+    nc = tc.nc
+    x_rows = x.flatten_outer_dims()
+    kf_rows = out_0.rearrange("b s h d -> (b s) (h d)")
+    v_rows = out_1.rearrange("b s h d -> (b s) (h d)")
+
+    with ExitStack() as ctx:
+        const = ctx.enter_context(tc.tile_pool(name="const", bufs=1))
+        raw = ctx.enter_context(tc.tile_pool(name="raw", bufs=1))
+        stage = ctx.enter_context(tc.tile_pool(name="stage", bufs=3))
+        x_pool = ctx.enter_context(tc.tile_pool(name="x_pool", bufs=2))
+        c_pool = ctx.enter_context(tc.tile_pool(name="c_pool", bufs=3))
+        rope_pool = ctx.enter_context(tc.tile_pool(name="rope_pool", bufs=2))
+        out_pool = ctx.enter_context(tc.tile_pool(name="out_pool", bufs=2))
+        psum_x = ctx.enter_context(tc.psum_pool(name="psum_x", bufs=2))
+        psum_c = ctx.enter_context(tc.psum_pool(name="psum_c", bufs=1))
+        psum_kv = ctx.enter_context(tc.psum_pool(name="psum_kv", bufs=4))
+
+        x_raw = [raw.tile([P, D_MODEL], BF16, name="x_raw%d" % i) for i in range(TOKEN_TILES)]
+        wa_raw = raw.tile([P, X_PASSES, PACK, LATENT + ROPE], BF16)
+        wb_raw = raw.tile([P, WB_PIECES, PACK, HEADS // WB_PIECES * (NOPE + VDIM)], BF16)
+        nc.sync.dma_start(out=x_raw[0][:], in_=x_rows[span(0, P), :])
+        for g in range(X_PASSES):
+            nc.sync.dma_start(
+                out=wa_raw[:, g, :, :], in_=Wkva[span(g, K_PASS), :].rearrange("(p j) c -> p j c", j=PACK)
+            )
+        wb_by_partition = Wkvb.rearrange("(p t) n -> p t n", p=P)
+        for piece in range(WB_PIECES):
+            nc.sync.dma_start(
+                out=wb_raw[:, piece, :, :],
+                in_=wb_by_partition[:, :, span(piece, HEADS // WB_PIECES * (NOPE + VDIM))],
+            )
+        for i in range(1, TOKEN_TILES):
+            nc.sync.dma_start(out=x_raw[i][:], in_=x_rows[span(i, P), :])
+
+        ident = const.tile([P, P], F32)
+        make_identity(nc, ident[:])
+
+        freq = const.tile([P, PAIRS], F32)
+        nc.vector.memset(freq[:, 0:1], 1.0)
+        for doubling in range(6):
+            w = 2**doubling
+            nc.vector.tensor_scalar(
+                out=freq[:, w : 2 * w],
+                in0=freq[:, 0:w],
+                scalar1=ROPE_BASE ** (-2.0 * w / ROPE),
+                scalar2=None,
+                op0=ALU.mult,
+            )
+        position = const.tile([P, 2], F32)
+        nc.gpsimd.iota(
+            position[:], pattern=[[P, 2]], base=0, channel_multiplier=1, allow_small_or_imprecise_dtypes=True
+        )
+        turns = const.tile([P, 2 * 2 * PAIRS], F32)
+        turns_view = turns[:].rearrange("p (f h j) -> p f h j", f=2, h=2)
+        for half in range(2):
+            nc.vector.tensor_scalar(
+                out=turns_view[:, 0, half, :],
+                in0=freq[:],
+                scalar1=position[:, half : half + 1],
+                scalar2=1.0 / (2.0 * math.pi),
+                op0=ALU.mult,
+                op1=ALU.mult,
+            )
+        nc.vector.tensor_scalar(
+            out=turns[:, 2 * PAIRS :], in0=turns[:, : 2 * PAIRS], scalar1=0.25, scalar2=None, op0=ALU.add
+        )
+        whole_turns = const.tile([P, 2 * 2 * PAIRS], F32)
+        nc.vector.tensor_scalar(
+            out=whole_turns[:],
+            in0=turns[:],
+            scalar1=ROUND_MAGIC,
+            scalar2=ROUND_MAGIC,
+            op0=ALU.add,
+            op1=ALU.subtract,
+        )
+        part_turns = const.tile([P, 2 * 2 * PAIRS], F32)
+        nc.vector.tensor_tensor(out=part_turns[:], in0=turns[:], in1=whole_turns[:], op=ALU.subtract)
+        trig = const.tile([P, 2 * 2 * PAIRS], F32)
+        nc.scalar.activation(
+            out=trig[:], in_=part_turns[:], func=mybir.ActivationFunctionType.Sin, scale=2.0 * math.pi
+        )
+        trig_view = trig[:].rearrange("p (f h j) -> p f h j", f=2, h=2)
+
+        wa_codes = const.tile([P, X_PASSES * LATENT], U32, align_bytes=64)
+        wa_scales = const.tile([P, X_PASSES * LATENT], U8, align_bytes=64)
+        wr_codes = const.tile([P, X_PASSES * ROPE], U32, align_bytes=64)
+        wr_scales = const.tile([P, X_PASSES * ROPE], U8, align_bytes=64)
+        wb_codes = const.tile([P, 2 * HEADS * NOPE], U32, align_bytes=64)
+        wb_scales = const.tile([P, 2 * HEADS * NOPE], U8, align_bytes=64)
+
+        def quantise_unit(columns, codes, scales):
+            grouped = stage.tile([P, UNIT], BF16, align_bytes=64)
+            target = grouped[:].rearrange("p (n c i j) -> p n c j i", n=4, i=RUN, j=PACK)
+            source = columns.rearrange("p n (c i) j -> p n c j i", i=RUN)
+            nc.vector.tensor_copy(out=target[:, 0:2], in_=source[:, 0:2])
+            for n in range(2, 4):
+                nc.scalar.copy(out=target[:, n], in_=source[:, n])
+            nc.vector.quantize_mx(out=codes.bitcast(FP8X4), scales=scales, in_=grouped[:])
+
+        def quantise_wkva():
+            for g in range(X_PASSES):
+                grouped = stage.tile([P, UNIT], BF16, align_bytes=64)
+                target = grouped[:].rearrange("p (t m j) -> p t m j", t=PACK, j=PACK)
+                source = wa_raw[:, g, :, :LATENT].rearrange("p j (m t) -> p t m j", t=PACK)
+                nc.vector.tensor_copy(out=target[:, 0:2], in_=source[:, 0:2])
+                for t in range(2, 4):
+                    nc.scalar.copy(out=target[:, t], in_=source[:, t])
+                nc.vector.quantize_mx(
+                    out=wa_codes[:, span(g, LATENT)].bitcast(FP8X4), scales=wa_scales[:, span(g, LATENT)], in_=grouped[:]
+                )
+            quantise_unit(wa_raw[:, :, :, LATENT:].rearrange("p g j c -> p g c j"), wr_codes[:], wr_scales[:])
+
+        def quantise_wkvb():
+            groups = HEAD_GROUPS // WB_PIECES
+            for kind in range(2):
+                for q in range(HEAD_GROUPS):
+                    heads = wb_raw[:, q // groups, :, :].rearrange("p t (h k c) -> p k h c t", k=2, c=NOPE)
+                    quantise_unit(
+                        heads[:, kind, span(q % groups, HEAD_GROUP)],
+                        wb_codes[:, span(kind * HEAD_GROUPS + q, BANK)],
+                        wb_scales[:, span(kind * HEAD_GROUPS + q, BANK)],
+                    )
+
+        x_quantised = {}
+        c_quantised = {}
+        kf_tiles = {}
+
+        def prepare(i):
+            words = x_raw[i][:].bitcast(F32).rearrange("r (g p u) -> r g u p", g=X_PASSES, u=2)
+            x_grouped = x_pool.tile([P, D_MODEL], BF16, align_bytes=64)
+            grouped_words = x_grouped[:].bitcast(F32).rearrange("p (g r u) -> p g r u", g=X_PASSES, u=2)
+            for bank in range(2):
+                x_t = psum_x.tile([P, 2, 2, P], F32)
+                for g in range(2):
+                    for u in range(2):
+                        nc.tensor.transpose(out=x_t[:, g, u, :], in_=words[:, 2 * bank + g, u, :], identity=ident[:])
+                nc.vector.tensor_copy(
+                    out=grouped_words[:, span(bank, 2), :, :], in_=x_t[:].rearrange("p g u r -> p g r u")
+                )
+            x_codes = x_pool.tile([P, X_PASSES * P], U32, align_bytes=64)
+            x_scales = x_pool.tile([P, X_PASSES * P], U8, align_bytes=64)
+            nc.vector.quantize_mx(out=x_codes[:].bitcast(FP8X4), scales=x_scales[:], in_=x_grouped[:])
+            x_quantised[i] = (x_codes, x_scales)
+
+        def project(i):
+            x_codes, x_scales = x_quantised[i]
+            c_t = psum_c.tile([P, PACK, P], F32)
+            for t in range(PACK):
+                for g in range(X_PASSES):
+                    nc.tensor.matmul_mx(
+                        out=c_t[:, t, :],
+                        lhsT=wa_codes[:, span(g * PACK + t, P)].bitcast(FP8X4),
+                        lhsT_scale=wa_scales[:, span(g * PACK + t, P)],
+                        rhs=x_codes[:, span(g, P)].bitcast(FP8X4),
+                        rhs_scale=x_scales[:, span(g, P)],
+                        start=(g == 0),
+                        stop=(g == X_PASSES - 1),
+                    )
+            k_pe = psum_c.tile([P, ROPE], F32)
+            for g in range(X_PASSES):
+                nc.tensor.matmul_mx(
+                    out=k_pe[:],
+                    lhsT=x_codes[:, span(g, P)].bitcast(FP8X4),
+                    lhsT_scale=x_scales[:, span(g, P)],
+                    rhs=wr_codes[:, span(g, ROPE)].bitcast(FP8X4),
+                    rhs_scale=wr_scales[:, span(g, ROPE)],
+                    start=(g == 0),
+                    stop=(g == X_PASSES - 1),
+                )
+            c_grouped = c_pool.tile([P, P, PACK], BF16, align_bytes=64)
+            nc.vector.tensor_copy(out=c_grouped[:], in_=c_t[:].rearrange("p t r -> p r t"))
+            c_codes = c_pool.tile([P, P], U32, align_bytes=64)
+            c_scales = c_pool.tile([P, P], U8, align_bytes=64)
+            nc.vector.quantize_mx(
+                out=c_codes[:].bitcast(FP8X4), scales=c_scales[:], in_=c_grouped[:].rearrange("p r t -> p (r t)")
+            )
+            c_quantised[i] = (c_codes, c_scales)
+
+            half = i % 2
+            sin = trig_view[:, 0, half, :].unsqueeze(2).to_broadcast([P, PAIRS, 2])
+            cos = trig_view[:, 1, half, :].unsqueeze(2).to_broadcast([P, PAIRS, 2])
+            pairs = k_pe[:].rearrange("p (j e) -> p j e", e=2)
+            by_cos = rope_pool.tile([P, PAIRS, 2], F32)
+            by_sin = rope_pool.tile([P, PAIRS, 2], F32)
+            rotated = rope_pool.tile([P, PAIRS, 2], F32)
+            nc.vector.tensor_tensor(out=by_cos[:], in0=pairs, in1=cos, op=ALU.mult)
+            nc.vector.tensor_tensor(out=by_sin[:], in0=pairs, in1=sin, op=ALU.mult)
+            nc.vector.tensor_tensor(out=rotated[:, :, 0], in0=by_cos[:, :, 0], in1=by_sin[:, :, 1], op=ALU.subtract)
+            nc.vector.tensor_tensor(out=rotated[:, :, 1], in0=by_sin[:, :, 0], in1=by_cos[:, :, 1], op=ALU.add)
+            kf_tile = out_pool.tile([P, HEADS, NOPE + ROPE], F32, bufs=3)
+            nc.vector.tensor_copy(
+                out=kf_tile[:, :, NOPE:],
+                in_=rotated[:].rearrange("p j e -> p (j e)").unsqueeze(1).to_broadcast([P, HEADS, ROPE]),
+            )
+            kf_tiles[i] = kf_tile
+
+        def expand(i):
+            c_codes, c_scales = c_quantised[i]
+            kf_tile = kf_tiles[i]
+            v_tile = out_pool.tile([P, HEADS, VDIM], F32)
+            for kind in range(2):
+                for q in range(HEAD_GROUPS):
+                    kv = psum_kv.tile([P, HEAD_GROUP, NOPE], F32)
+                    nc.tensor.matmul_mx(
+                        out=kv[:].rearrange("p h c -> p (h c)"),
+                        lhsT=c_codes[:].bitcast(FP8X4),
+                        lhsT_scale=c_scales[:],
+                        rhs=wb_codes[:, span(kind * HEAD_GROUPS + q, BANK)].bitcast(FP8X4),
+                        rhs_scale=wb_scales[:, span(kind * HEAD_GROUPS + q, BANK)],
+                        start=True,
+                        stop=True,
+                    )
+                    if kind == 0:
+                        nc.scalar.copy(out=kf_tile[:, span(q, HEAD_GROUP), :NOPE], in_=kv[:])
+                    else:
+                        nc.scalar.copy(out=v_tile[:, span(q, HEAD_GROUP), :], in_=kv[:])
+                if kind == 0:
+                    nc.sync.dma_start(out=kf_rows[span(i, P), :], in_=kf_tile[:].rearrange("p h d -> p (h d)"))
+                else:
+                    nc.sync.dma_start(out=v_rows[span(i, P), :], in_=v_tile[:].rearrange("p h d -> p (h d)"))
+
+        prepare(0)
+        quantise_wkva()
+        project(0)
+        prepare(1)
+        quantise_wkvb()
+        for i in range(TOKEN_TILES):
+            if i + 2 < TOKEN_TILES:
+                prepare(i + 2)
+            if i + 1 < TOKEN_TILES:
+                project(i + 1)
+            expand(i)

@@ -33,7 +33,7 @@ HEAD_GROUP = BANK // NOPE
 HEAD_GROUPS = HEADS // HEAD_GROUP
 UNIT = BANK * PACK
 RUN = 4
-WB_PIECES = 2
+BATCHES = 4
 ROUND_MAGIC = 1.5 * 2.0**23
 
 FLOPS = 2 * TOKENS * D_MODEL * (LATENT + ROPE) + 2 * TOKENS * LATENT * HEADS * (NOPE + VDIM)
@@ -45,9 +45,9 @@ def span(index, width):
 
 def tile_multilatentattention_pb_kernel(tc, x, Wkva, Wkvb, out_0, out_1):
     nc = tc.nc
-    x_rows = x.flatten_outer_dims()
-    kf_rows = out_0.rearrange("b s h d -> (b s) (h d)")
-    v_rows = out_1.rearrange("b s h d -> (b s) (h d)")
+    x_batches = x.rearrange("b (p e) k -> b p e k", e=2)
+    kf_rows = out_0.rearrange("b (p e) h d -> b e p (h d)", e=2)
+    v_rows = out_1.rearrange("b (p e) h d -> b e p (h d)", e=2)
 
     with ExitStack() as ctx:
         const = ctx.enter_context(tc.tile_pool(name="const", bufs=1))
@@ -56,30 +56,42 @@ def tile_multilatentattention_pb_kernel(tc, x, Wkva, Wkvb, out_0, out_1):
         x_pool = ctx.enter_context(tc.tile_pool(name="x_pool", bufs=2))
         c_pool = ctx.enter_context(tc.tile_pool(name="c_pool", bufs=3))
         rope_pool = ctx.enter_context(tc.tile_pool(name="rope_pool", bufs=2))
-        out_pool = ctx.enter_context(tc.tile_pool(name="out_pool", bufs=2))
+        out_pool = ctx.enter_context(tc.tile_pool(name="out_pool", bufs=3))
         psum_x = ctx.enter_context(tc.psum_pool(name="psum_x", bufs=2))
         psum_c = ctx.enter_context(tc.psum_pool(name="psum_c", bufs=1))
         psum_kv = ctx.enter_context(tc.psum_pool(name="psum_kv", bufs=4))
+        ctx.enter_context(tc.manual_schedule())
 
-        x_raw = [raw.tile([P, D_MODEL], BF16, name="x_raw%d" % i) for i in range(TOKEN_TILES)]
+        x_raw = [raw.tile([P, 2, D_MODEL], BF16, name="x_raw%d" % b) for b in range(BATCHES)]
         wa_raw = raw.tile([P, X_PASSES, PACK, LATENT + ROPE], BF16)
-        wb_raw = raw.tile([P, WB_PIECES, PACK, HEADS // WB_PIECES * (NOPE + VDIM)], BF16)
-        nc.sync.dma_start(out=x_raw[0][:], in_=x_rows[span(0, P), :])
-        for g in range(X_PASSES):
+        wb_raw = raw.tile([P, HEAD_GROUPS, PACK, HEAD_GROUP * (NOPE + VDIM)], BF16)
+
+        def load_wkva(g):
             nc.sync.dma_start(
                 out=wa_raw[:, g, :, :], in_=Wkva[span(g, K_PASS), :].rearrange("(p j) c -> p j c", j=PACK)
             )
-        wb_by_partition = Wkvb.rearrange("(p t) n -> p t n", p=P)
-        for piece in range(WB_PIECES):
+
+        wb_by_partition = Wkvb.rearrange("(p t) n -> p t n", t=PACK)
+        load_wkva(0)
+        load_wkva(1)
+        nc.sync.dma_start(out=x_raw[0][:, 0, :], in_=x_batches[0, :, 0, :])
+        load_wkva(2)
+        load_wkva(3)
+        for q in range(HEAD_GROUPS):
             nc.sync.dma_start(
-                out=wb_raw[:, piece, :, :],
-                in_=wb_by_partition[:, :, span(piece, HEADS // WB_PIECES * (NOPE + VDIM))],
+                out=wb_raw[:, q, :, :], in_=wb_by_partition[:, :, span(q, HEAD_GROUP * (NOPE + VDIM))]
             )
-        for i in range(1, TOKEN_TILES):
-            nc.sync.dma_start(out=x_raw[i][:], in_=x_rows[span(i, P), :])
+        nc.sync.dma_start(out=x_raw[0][:, 1, :], in_=x_batches[0, :, 1, :])
+        for b in range(1, BATCHES):
+            nc.sync.dma_start(out=x_raw[b][:], in_=x_batches[b])
 
         ident = const.tile([P, P], F32)
         make_identity(nc, ident[:])
+        first_sin = const.tile([P, 2], F32)
+        nc.vector.memset(first_sin[:, 0:1], 0.0)
+        nc.scalar.activation(
+            out=first_sin[:, 1:2], in_=first_sin[:, 0:1], func=mybir.ActivationFunctionType.Sin
+        )
 
         freq = const.tile([P, PAIRS], F32)
         nc.vector.memset(freq[:, 0:1], 1.0)
@@ -94,15 +106,15 @@ def tile_multilatentattention_pb_kernel(tc, x, Wkva, Wkvb, out_0, out_1):
             )
         position = const.tile([P, 2], F32)
         nc.gpsimd.iota(
-            position[:], pattern=[[P, 2]], base=0, channel_multiplier=1, allow_small_or_imprecise_dtypes=True
+            position[:], pattern=[[1, 2]], base=0, channel_multiplier=2, allow_small_or_imprecise_dtypes=True
         )
         turns = const.tile([P, 2 * 2 * PAIRS], F32)
         turns_view = turns[:].rearrange("p (f h j) -> p f h j", f=2, h=2)
-        for half in range(2):
+        for parity in range(2):
             nc.vector.tensor_scalar(
-                out=turns_view[:, 0, half, :],
+                out=turns_view[:, 0, parity, :],
                 in0=freq[:],
-                scalar1=position[:, half : half + 1],
+                scalar1=position[:, parity : parity + 1],
                 scalar2=1.0 / (2.0 * math.pi),
                 op0=ALU.mult,
                 op1=ALU.mult,
@@ -122,10 +134,12 @@ def tile_multilatentattention_pb_kernel(tc, x, Wkva, Wkvb, out_0, out_1):
         part_turns = const.tile([P, 2 * 2 * PAIRS], F32)
         nc.vector.tensor_tensor(out=part_turns[:], in0=turns[:], in1=whole_turns[:], op=ALU.subtract)
         trig = const.tile([P, 2 * 2 * PAIRS], F32)
-        nc.scalar.activation(
-            out=trig[:], in_=part_turns[:], func=mybir.ActivationFunctionType.Sin, scale=2.0 * math.pi
-        )
         trig_view = trig[:].rearrange("p (f h j) -> p f h j", f=2, h=2)
+
+        def take_sines():
+            nc.scalar.activation(
+                out=trig[:], in_=part_turns[:], func=mybir.ActivationFunctionType.Sin, scale=2.0 * math.pi
+            )
 
         wa_codes = const.tile([P, X_PASSES * LATENT], U32, align_bytes=64)
         wa_scales = const.tile([P, X_PASSES * LATENT], U8, align_bytes=64)
@@ -134,64 +148,75 @@ def tile_multilatentattention_pb_kernel(tc, x, Wkva, Wkvb, out_0, out_1):
         wb_codes = const.tile([P, 2 * HEADS * NOPE], U32, align_bytes=64)
         wb_scales = const.tile([P, 2 * HEADS * NOPE], U8, align_bytes=64)
 
-        def quantise_unit(columns, codes, scales):
+        units = []
+        for g in range(X_PASSES):
+            units.append((None, wa_codes[:, span(g, LATENT)], wa_scales[:, span(g, LATENT)]))
+        units.append((wa_raw[:, :, :, LATENT:].rearrange("p g j c -> p g c j"), wr_codes[:], wr_scales[:]))
+        for kind in range(2):
+            for q in range(HEAD_GROUPS):
+                heads = wb_raw[:, q, :, :].rearrange("p t (h k c) -> p k h c t", k=2, c=NOPE)
+                columns = span(kind * HEAD_GROUPS + q, BANK)
+                units.append((heads[:, kind], wb_codes[:, columns], wb_scales[:, columns]))
+        unit_tiles = {}
+
+        def regroup(n):
             grouped = stage.tile([P, UNIT], BF16, align_bytes=64)
-            target = grouped[:].rearrange("p (n c i j) -> p n c j i", n=4, i=RUN, j=PACK)
-            source = columns.rearrange("p n (c i) j -> p n c j i", i=RUN)
-            nc.vector.tensor_copy(out=target[:, 0:2], in_=source[:, 0:2])
-            for n in range(2, 4):
-                nc.scalar.copy(out=target[:, n], in_=source[:, n])
-            nc.vector.quantize_mx(out=codes.bitcast(FP8X4), scales=scales, in_=grouped[:])
-
-        def quantise_wkva():
-            for g in range(X_PASSES):
-                grouped = stage.tile([P, UNIT], BF16, align_bytes=64)
+            unit_tiles[n] = grouped
+            if n < X_PASSES:
                 target = grouped[:].rearrange("p (t m j) -> p t m j", t=PACK, j=PACK)
-                source = wa_raw[:, g, :, :LATENT].rearrange("p j (m t) -> p t m j", t=PACK)
+                source = wa_raw[:, n, :, :LATENT].rearrange("p j (m t) -> p t m j", t=PACK)
                 nc.vector.tensor_copy(out=target[:, 0:2], in_=source[:, 0:2])
-                for t in range(2, 4):
-                    nc.scalar.copy(out=target[:, t], in_=source[:, t])
-                nc.vector.quantize_mx(
-                    out=wa_codes[:, span(g, LATENT)].bitcast(FP8X4), scales=wa_scales[:, span(g, LATENT)], in_=grouped[:]
-                )
-            quantise_unit(wa_raw[:, :, :, LATENT:].rearrange("p g j c -> p g c j"), wr_codes[:], wr_scales[:])
+                nc.scalar.copy(out=target[:, 2:4], in_=source[:, 2:4])
+            else:
+                target = grouped[:].rearrange("p (n c i j) -> p n c j i", n=4, i=RUN, j=PACK)
+                source = units[n][0].rearrange("p n (c i) j -> p n c j i", i=RUN)
+                shared = 1 if n in (9, 10) else 2
+                nc.vector.tensor_copy(out=target[:, :shared], in_=source[:, :shared])
+                for block in range(shared, 4):
+                    nc.scalar.copy(out=target[:, block], in_=source[:, block])
 
-        def quantise_wkvb():
-            groups = HEAD_GROUPS // WB_PIECES
-            for kind in range(2):
-                for q in range(HEAD_GROUPS):
-                    heads = wb_raw[:, q // groups, :, :].rearrange("p t (h k c) -> p k h c t", k=2, c=NOPE)
-                    quantise_unit(
-                        heads[:, kind, span(q % groups, HEAD_GROUP)],
-                        wb_codes[:, span(kind * HEAD_GROUPS + q, BANK)],
-                        wb_scales[:, span(kind * HEAD_GROUPS + q, BANK)],
-                    )
+        def quantise(n):
+            nc.vector.quantize_mx(out=units[n][1].bitcast(FP8X4), scales=units[n][2], in_=unit_tiles[n][:])
 
+        x_banks = {}
+        x_tiles = {}
         x_quantised = {}
+        c_banks = {}
+        k_pe_banks = {}
+        c_tiles = {}
         c_quantised = {}
+        rope_tiles = {}
         kf_tiles = {}
+        v_tiles = {}
 
-        def prepare(i):
-            words = x_raw[i][:].bitcast(F32).rearrange("r (g p u) -> r g u p", g=X_PASSES, u=2)
-            x_grouped = x_pool.tile([P, D_MODEL], BF16, align_bytes=64)
-            grouped_words = x_grouped[:].bitcast(F32).rearrange("p (g r u) -> p g r u", g=X_PASSES, u=2)
+        def transpose_x(i):
+            words = x_raw[i // 2][:, i % 2, :].bitcast(F32).rearrange("r (g p u) -> r g u p", g=X_PASSES, u=2)
             for bank in range(2):
                 x_t = psum_x.tile([P, 2, 2, P], F32)
                 for g in range(2):
                     for u in range(2):
                         nc.tensor.transpose(out=x_t[:, g, u, :], in_=words[:, 2 * bank + g, u, :], identity=ident[:])
-                nc.vector.tensor_copy(
-                    out=grouped_words[:, span(bank, 2), :, :], in_=x_t[:].rearrange("p g u r -> p g r u")
-                )
+                x_banks[i, bank] = x_t
+            x_grouped = x_pool.tile([P, D_MODEL], BF16, align_bytes=64)
+            x_tiles[i] = x_grouped
+
+        def gather_x(i, bank, copy):
+            words = x_tiles[i][:].bitcast(F32).rearrange("p (g r u) -> p g r u", g=X_PASSES, u=2)
+            copy(out=words[:, span(bank, 2), :, :], in_=x_banks[i, bank][:].rearrange("p g u r -> p g r u"))
+
+        def quantise_x(i):
             x_codes = x_pool.tile([P, X_PASSES * P], U32, align_bytes=64)
             x_scales = x_pool.tile([P, X_PASSES * P], U8, align_bytes=64)
-            nc.vector.quantize_mx(out=x_codes[:].bitcast(FP8X4), scales=x_scales[:], in_=x_grouped[:])
+            nc.vector.quantize_mx(out=x_codes[:].bitcast(FP8X4), scales=x_scales[:], in_=x_tiles[i][:])
             x_quantised[i] = (x_codes, x_scales)
 
-        def project(i):
+        def project_c(i, pieces):
             x_codes, x_scales = x_quantised[i]
-            c_t = psum_c.tile([P, PACK, P], F32)
-            for t in range(PACK):
+            if pieces[0] == 0:
+                c_t = psum_c.tile([P, PACK, P], F32)
+                c_banks[i] = c_t
+            c_t = c_banks[i]
+            for t in pieces:
                 for g in range(X_PASSES):
                     nc.tensor.matmul_mx(
                         out=c_t[:, t, :],
@@ -202,6 +227,9 @@ def tile_multilatentattention_pb_kernel(tc, x, Wkva, Wkvb, out_0, out_1):
                         start=(g == 0),
                         stop=(g == X_PASSES - 1),
                     )
+
+        def project_rope(i):
+            x_codes, x_scales = x_quantised[i]
             k_pe = psum_c.tile([P, ROPE], F32)
             for g in range(X_PASSES):
                 nc.tensor.matmul_mx(
@@ -213,66 +241,178 @@ def tile_multilatentattention_pb_kernel(tc, x, Wkva, Wkvb, out_0, out_1):
                     start=(g == 0),
                     stop=(g == X_PASSES - 1),
                 )
+            k_pe_banks[i] = k_pe
+
+        def project(i):
+            project_c(i, (0, 1, 2, 3))
+            project_rope(i)
+
+        def gather_c(i):
             c_grouped = c_pool.tile([P, P, PACK], BF16, align_bytes=64)
-            nc.vector.tensor_copy(out=c_grouped[:], in_=c_t[:].rearrange("p t r -> p r t"))
+            nc.vector.tensor_copy(out=c_grouped[:], in_=c_banks[i][:].rearrange("p t r -> p r t"))
+            c_tiles[i] = c_grouped
+
+        def quantise_c(i):
             c_codes = c_pool.tile([P, P], U32, align_bytes=64)
             c_scales = c_pool.tile([P, P], U8, align_bytes=64)
             nc.vector.quantize_mx(
-                out=c_codes[:].bitcast(FP8X4), scales=c_scales[:], in_=c_grouped[:].rearrange("p r t -> p (r t)")
+                out=c_codes[:].bitcast(FP8X4), scales=c_scales[:], in_=c_tiles[i][:].rearrange("p r t -> p (r t)")
             )
             c_quantised[i] = (c_codes, c_scales)
 
-            half = i % 2
-            sin = trig_view[:, 0, half, :].unsqueeze(2).to_broadcast([P, PAIRS, 2])
-            cos = trig_view[:, 1, half, :].unsqueeze(2).to_broadcast([P, PAIRS, 2])
-            pairs = k_pe[:].rearrange("p (j e) -> p j e", e=2)
+        def rope_products(i):
+            sin = trig_view[:, 0, i % 2, :].unsqueeze(2).to_broadcast([P, PAIRS, 2])
+            cos = trig_view[:, 1, i % 2, :].unsqueeze(2).to_broadcast([P, PAIRS, 2])
+            pairs = k_pe_banks[i][:].rearrange("p (j e) -> p j e", e=2)
             by_cos = rope_pool.tile([P, PAIRS, 2], F32)
             by_sin = rope_pool.tile([P, PAIRS, 2], F32)
-            rotated = rope_pool.tile([P, PAIRS, 2], F32)
             nc.vector.tensor_tensor(out=by_cos[:], in0=pairs, in1=cos, op=ALU.mult)
             nc.vector.tensor_tensor(out=by_sin[:], in0=pairs, in1=sin, op=ALU.mult)
+            rope_tiles[i] = (by_cos, by_sin)
+
+        def rope_sums(i):
+            by_cos, by_sin = rope_tiles[i]
+            rotated = rope_pool.tile([P, PAIRS, 2], F32)
             nc.vector.tensor_tensor(out=rotated[:, :, 0], in0=by_cos[:, :, 0], in1=by_sin[:, :, 1], op=ALU.subtract)
             nc.vector.tensor_tensor(out=rotated[:, :, 1], in0=by_sin[:, :, 0], in1=by_cos[:, :, 1], op=ALU.add)
-            kf_tile = out_pool.tile([P, HEADS, NOPE + ROPE], F32, bufs=3)
+            rope_tiles[i] = rotated
+
+        def kf_tile_of(i):
+            if i not in kf_tiles:
+                kf_tile = out_pool.tile([P, HEADS, NOPE + ROPE], F32)
+                kf_tiles[i] = kf_tile
+            return kf_tiles[i]
+
+        def spread_rope(i):
             nc.vector.tensor_copy(
-                out=kf_tile[:, :, NOPE:],
-                in_=rotated[:].rearrange("p j e -> p (j e)").unsqueeze(1).to_broadcast([P, HEADS, ROPE]),
+                out=kf_tile_of(i)[:, :, NOPE:],
+                in_=rope_tiles[i][:].rearrange("p j e -> p (j e)").unsqueeze(1).to_broadcast([P, HEADS, ROPE]),
             )
-            kf_tiles[i] = kf_tile
 
-        def expand(i):
+        kv_banks = {}
+
+        def expand(i, kind, q):
             c_codes, c_scales = c_quantised[i]
-            kf_tile = kf_tiles[i]
-            v_tile = out_pool.tile([P, HEADS, VDIM], F32)
-            for kind in range(2):
-                for q in range(HEAD_GROUPS):
-                    kv = psum_kv.tile([P, HEAD_GROUP, NOPE], F32)
-                    nc.tensor.matmul_mx(
-                        out=kv[:].rearrange("p h c -> p (h c)"),
-                        lhsT=c_codes[:].bitcast(FP8X4),
-                        lhsT_scale=c_scales[:],
-                        rhs=wb_codes[:, span(kind * HEAD_GROUPS + q, BANK)].bitcast(FP8X4),
-                        rhs_scale=wb_scales[:, span(kind * HEAD_GROUPS + q, BANK)],
-                        start=True,
-                        stop=True,
-                    )
-                    if kind == 0:
-                        nc.scalar.copy(out=kf_tile[:, span(q, HEAD_GROUP), :NOPE], in_=kv[:])
-                    else:
-                        nc.scalar.copy(out=v_tile[:, span(q, HEAD_GROUP), :], in_=kv[:])
-                if kind == 0:
-                    nc.sync.dma_start(out=kf_rows[span(i, P), :], in_=kf_tile[:].rearrange("p h d -> p (h d)"))
-                else:
-                    nc.sync.dma_start(out=v_rows[span(i, P), :], in_=v_tile[:].rearrange("p h d -> p (h d)"))
+            kv = psum_kv.tile([P, HEAD_GROUP, NOPE], F32)
+            nc.tensor.matmul_mx(
+                out=kv[:].rearrange("p h c -> p (h c)"),
+                lhsT=c_codes[:].bitcast(FP8X4),
+                lhsT_scale=c_scales[:],
+                rhs=wb_codes[:, span(kind * HEAD_GROUPS + q, BANK)].bitcast(FP8X4),
+                rhs_scale=wb_scales[:, span(kind * HEAD_GROUPS + q, BANK)],
+                start=True,
+                stop=True,
+            )
+            kv_banks[i, kind, q] = kv
 
-        prepare(0)
-        quantise_wkva()
+        def empty(i, kind, q):
+            if kind == 0:
+                nc.scalar.copy(out=kf_tile_of(i)[:, span(q, HEAD_GROUP), :NOPE], in_=kv_banks[i, 0, q][:])
+            else:
+                if q == 0:
+                    v_tile = out_pool.tile([P, HEADS, VDIM], F32)
+                    v_tiles[i] = v_tile
+                nc.scalar.copy(out=v_tiles[i][:, span(q, HEAD_GROUP), :], in_=kv_banks[i, 1, q][:])
+
+        def store(i, kind):
+            if kind == 0:
+                nc.sync.dma_start(out=kf_rows[i // 2, i % 2], in_=kf_tiles[i][:].rearrange("p h d -> p (h d)"))
+            else:
+                nc.sync.dma_start(out=v_rows[i // 2, i % 2], in_=v_tiles[i][:].rearrange("p h d -> p (h d)"))
+
+        by_vector, by_scalar = nc.vector.tensor_copy, nc.scalar.copy
+        regroup(0)
+        regroup(1)
+        transpose_x(0)
+        quantise(0)
+        take_sines()
+        gather_x(0, 0, by_vector)
+        gather_x(0, 1, by_scalar)
+        regroup(2)
+        quantise(1)
+        quantise_x(0)
+        regroup(3)
+        quantise(2)
+        regroup(4)
+        quantise(3)
+        regroup(5)
+        quantise(4)
         project(0)
-        prepare(1)
-        quantise_wkvb()
-        for i in range(TOKEN_TILES):
-            if i + 2 < TOKEN_TILES:
-                prepare(i + 2)
+        regroup(9)
+        quantise(5)
+        gather_c(0)
+        regroup(6)
+        rope_products(0)
+        quantise_c(0)
+        quantise(9)
+        expand(0, 0, 0)
+        rope_sums(0)
+        regroup(7)
+        empty(0, 0, 0)
+        quantise(6)
+        expand(0, 0, 1)
+        regroup(10)
+        quantise(7)
+        expand(0, 0, 2)
+        empty(0, 0, 1)
+        regroup(8)
+        quantise(10)
+        empty(0, 0, 2)
+        regroup(11)
+        quantise(8)
+        expand(0, 0, 3)
+        transpose_x(1)
+        spread_rope(0)
+        empty(0, 0, 3)
+        store(0, 0)
+        gather_x(1, 0, by_scalar)
+        regroup(12)
+        quantise(11)
+        gather_x(1, 1, by_scalar)
+        transpose_x(2)
+        quantise_x(1)
+        for q in range(3):
+            expand(0, 1, q)
+            empty(0, 1, q)
+        project(1)
+        quantise(12)
+        expand(0, 1, 3)
+        empty(0, 1, 3)
+        store(0, 1)
+        gather_c(1)
+        rope_products(1)
+        quantise_c(1)
+        rope_sums(1)
+        gather_x(2, 0, by_vector)
+        spread_rope(1)
+        gather_x(2, 1, by_vector)
+        quantise_x(2)
+        transpose_x(3)
+
+        for i in range(1, TOKEN_TILES):
+            for q in range(HEAD_GROUPS):
+                expand(i, 0, q)
+                empty(i, 0, q)
+                if i + 2 < TOKEN_TILES and q < 2:
+                    gather_x(i + 2, q, by_vector)
+                if i + 1 < TOKEN_TILES and q == 1:
+                    project_c(i + 1, (0, 1))
+            store(i, 0)
             if i + 1 < TOKEN_TILES:
-                project(i + 1)
-            expand(i)
+                project_c(i + 1, (2, 3))
+                project_rope(i + 1)
+                gather_c(i + 1)
+                rope_products(i + 1)
+            if i + 2 < TOKEN_TILES:
+                quantise_x(i + 2)
+            if i + 1 < TOKEN_TILES:
+                quantise_c(i + 1)
+                rope_sums(i + 1)
+            for q in range(HEAD_GROUPS):
+                expand(i, 1, q)
+                empty(i, 1, q)
+            store(i, 1)
+            if i + 1 < TOKEN_TILES:
+                spread_rope(i + 1)
+            if i + 3 < TOKEN_TILES:
+                transpose_x(i + 3)

@@ -74,14 +74,14 @@ def tile_multilatentattention_pb_kernel(tc, x, Wkva, Wkvb, out_0, out_1):
         wb_by_partition = Wkvb.rearrange("(p t) n -> p t n", t=PACK)
         load_wkva(0)
         load_wkva(1)
-        nc.sync.dma_start(out=x_raw[0][:, 0, :], in_=x_batches[0, :, 0, :])
         load_wkva(2)
+        nc.sync.dma_start(out=x_raw[0][:, 0, :], in_=x_batches[0, :, 0, :])
         load_wkva(3)
+        nc.sync.dma_start(out=x_raw[0][:, 1, :], in_=x_batches[0, :, 1, :])
         for q in range(HEAD_GROUPS):
             nc.sync.dma_start(
                 out=wb_raw[:, q, :, :], in_=wb_by_partition[:, :, span(q, HEAD_GROUP * (NOPE + VDIM))]
             )
-        nc.sync.dma_start(out=x_raw[0][:, 1, :], in_=x_batches[0, :, 1, :])
         for b in range(1, BATCHES):
             nc.sync.dma_start(out=x_raw[b][:], in_=x_batches[b])
 
@@ -165,14 +165,13 @@ def tile_multilatentattention_pb_kernel(tc, x, Wkva, Wkvb, out_0, out_1):
             if n < X_PASSES:
                 target = grouped[:].rearrange("p (t m j) -> p t m j", t=PACK, j=PACK)
                 source = wa_raw[:, n, :, :LATENT].rearrange("p j (m t) -> p t m j", t=PACK)
-                nc.vector.tensor_copy(out=target[:, 0:2], in_=source[:, 0:2])
-                nc.scalar.copy(out=target[:, 2:4], in_=source[:, 2:4])
+                nc.vector.tensor_copy(out=target[:, :2], in_=source[:, :2])
+                nc.scalar.copy(out=target[:, 2:], in_=source[:, 2:])
             else:
                 target = grouped[:].rearrange("p (n c i j) -> p n c j i", n=4, i=RUN, j=PACK)
                 source = units[n][0].rearrange("p n (c i) j -> p n c j i", i=RUN)
-                shared = 1 if n in (9, 10) else 2
-                nc.vector.tensor_copy(out=target[:, :shared], in_=source[:, :shared])
-                for block in range(shared, 4):
+                nc.vector.tensor_copy(out=target[:, :2], in_=source[:, :2])
+                for block in range(2, 4):
                     nc.scalar.copy(out=target[:, block], in_=source[:, block])
 
         def quantise(n):
@@ -326,70 +325,102 @@ def tile_multilatentattention_pb_kernel(tc, x, Wkva, Wkvb, out_0, out_1):
         transpose_x(0)
         quantise(0)
         take_sines()
-        gather_x(0, 0, by_vector)
-        gather_x(0, 1, by_scalar)
         regroup(2)
         quantise(1)
-        quantise_x(0)
+        gather_x(0, 0, by_vector)
+        gather_x(0, 1, by_scalar)
         regroup(3)
+        quantise_x(0)
         quantise(2)
         regroup(4)
+        transpose_x(1)
         quantise(3)
+        gather_x(1, 1, by_scalar)
+        project_c(0, (0, 1, 2, 3))
         regroup(5)
         quantise(4)
-        project(0)
-        regroup(9)
+        project_rope(0)
+        regroup(6)
         quantise(5)
         gather_c(0)
-        regroup(6)
+        gather_x(1, 0, by_scalar)
+        regroup(7)
+        quantise(6)
         rope_products(0)
         quantise_c(0)
-        quantise(9)
-        expand(0, 0, 0)
         rope_sums(0)
-        regroup(7)
+        expand(0, 0, 0)
         empty(0, 0, 0)
-        quantise(6)
         expand(0, 0, 1)
-        regroup(10)
-        quantise(7)
-        expand(0, 0, 2)
-        empty(0, 0, 1)
+        quantise_x(1)
         regroup(8)
-        quantise(10)
-        empty(0, 0, 2)
-        regroup(11)
-        quantise(8)
-        expand(0, 0, 3)
-        transpose_x(1)
+        quantise(7)
+        empty(0, 0, 1)
+        expand(0, 0, 2)
         spread_rope(0)
+        project(1)
+        quantise(8)
+        regroup(9)
+        expand(0, 0, 3)
+        empty(0, 0, 2)
         empty(0, 0, 3)
         store(0, 0)
-        gather_x(1, 0, by_scalar)
-        regroup(12)
-        quantise(11)
-        gather_x(1, 1, by_scalar)
-        transpose_x(2)
-        quantise_x(1)
-        for q in range(3):
-            expand(0, 1, q)
-            empty(0, 1, q)
-        project(1)
-        quantise(12)
-        expand(0, 1, 3)
-        empty(0, 1, 3)
-        store(0, 1)
         gather_c(1)
+        transpose_x(2)
         rope_products(1)
         quantise_c(1)
         rope_sums(1)
+        expand(1, 0, 0)
+        expand(1, 0, 1)
         gather_x(2, 0, by_vector)
+        empty(1, 0, 0)
+        empty(1, 0, 1)
         spread_rope(1)
         gather_x(2, 1, by_vector)
+        expand(1, 0, 2)
+        expand(1, 0, 3)
+        empty(1, 0, 2)
+        empty(1, 0, 3)
+        store(1, 0)
+        quantise(9)
+        regroup(10)
         quantise_x(2)
+        quantise(10)
+        regroup(11)
+        expand(0, 1, 0)
+        project(2)
+        empty(0, 1, 0)
+        quantise(11)
+        regroup(12)
+        gather_c(2)
+        expand(0, 1, 1)
+        expand(0, 1, 2)
+        empty(0, 1, 1)
+        empty(0, 1, 2)
+        quantise(12)
+        rope_products(2)
+        quantise_c(2)
+        rope_sums(2)
         transpose_x(3)
+        expand(0, 1, 3)
+        empty(0, 1, 3)
+        store(0, 1)
+        spread_rope(2)
+        expand(1, 1, 0)
+        expand(1, 1, 1)
+        expand(1, 1, 2)
+        expand(1, 1, 3)
+        empty(1, 1, 0)
+        empty(1, 1, 1)
+        empty(1, 1, 2)
+        empty(1, 1, 3)
+        store(1, 1)
+        gather_x(3, 0, by_vector)
+        gather_x(3, 1, by_vector)
+        quantise_x(3)
+        transpose_x(4)
 
-        for i in range(1, TOKEN_TILES):
+        for i in range(2, TOKEN_TILES):
             for q in range(HEAD_GROUPS):
                 expand(i, 0, q)
                 empty(i, 0, q)

@@ -34,6 +34,7 @@ HEAD_GROUPS = HEADS // HEAD_GROUP
 UNIT = BANK * PACK
 RUN = 4
 BATCHES = 4
+PIECE = 4
 ROUND_MAGIC = 1.5 * 2.0**23
 
 FLOPS = 2 * TOKENS * D_MODEL * (LATENT + ROPE) + 2 * TOKENS * LATENT * HEADS * (NOPE + VDIM)
@@ -64,7 +65,7 @@ def tile_multilatentattention_pb_kernel(tc, x, Wkva, Wkvb, out_0, out_1):
 
         x_raw = [raw.tile([P, 2, D_MODEL], BF16, name="x_raw%d" % b) for b in range(BATCHES)]
         wa_raw = raw.tile([P, X_PASSES, PACK, LATENT + ROPE], BF16)
-        wb_raw = raw.tile([P, HEAD_GROUPS, PACK, HEAD_GROUP * (NOPE + VDIM)], BF16)
+        wb_raw = raw.tile([P, HEADS // PIECE, PACK, PIECE * (NOPE + VDIM)], BF16)
 
         def load_wkva(g):
             nc.sync.dma_start(
@@ -72,18 +73,27 @@ def tile_multilatentattention_pb_kernel(tc, x, Wkva, Wkvb, out_0, out_1):
             )
 
         wb_by_partition = Wkvb.rearrange("(p t) n -> p t n", t=PACK)
+        def load_wkvb(piece):
+            nc.sync.dma_start(
+                out=wb_raw[:, piece, :, :], in_=wb_by_partition[:, :, span(piece, PIECE * (NOPE + VDIM))]
+            )
+
+        def load_x(b, parities):
+            nc.sync.dma_start(out=x_raw[b][:, parities, :], in_=x_batches[b, :, parities, :])
+
         load_wkva(0)
         load_wkva(1)
         load_wkva(2)
-        nc.sync.dma_start(out=x_raw[0][:, 0, :], in_=x_batches[0, :, 0, :])
+        load_x(0, slice(0, 1))
         load_wkva(3)
-        nc.sync.dma_start(out=x_raw[0][:, 1, :], in_=x_batches[0, :, 1, :])
-        for q in range(HEAD_GROUPS):
-            nc.sync.dma_start(
-                out=wb_raw[:, q, :, :], in_=wb_by_partition[:, :, span(q, HEAD_GROUP * (NOPE + VDIM))]
-            )
-        for b in range(1, BATCHES):
-            nc.sync.dma_start(out=x_raw[b][:], in_=x_batches[b])
+        load_x(0, slice(1, 2))
+        load_wkvb(0)
+        load_wkvb(1)
+        load_wkvb(2)
+        load_wkvb(3)
+        load_x(1, slice(0, 2))
+        load_x(2, slice(0, 2))
+        load_x(3, slice(0, 2))
 
         ident = const.tile([P, P], F32)
         make_identity(nc, ident[:])
@@ -154,9 +164,10 @@ def tile_multilatentattention_pb_kernel(tc, x, Wkva, Wkvb, out_0, out_1):
         units.append((wa_raw[:, :, :, LATENT:].rearrange("p g j c -> p g c j"), wr_codes[:], wr_scales[:]))
         for kind in range(2):
             for q in range(HEAD_GROUPS):
-                heads = wb_raw[:, q, :, :].rearrange("p t (h k c) -> p k h c t", k=2, c=NOPE)
+                in_piece = q % (PIECE // HEAD_GROUP)
+                heads = wb_raw[:, q * HEAD_GROUP // PIECE, :, :].rearrange("p t (h k c) -> p k h c t", k=2, c=NOPE)
                 columns = span(kind * HEAD_GROUPS + q, BANK)
-                units.append((heads[:, kind], wb_codes[:, columns], wb_scales[:, columns]))
+                units.append((heads[:, kind, span(in_piece, HEAD_GROUP)], wb_codes[:, columns], wb_scales[:, columns]))
         unit_tiles = {}
 
         def regroup(n):
@@ -340,71 +351,73 @@ def tile_multilatentattention_pb_kernel(tc, x, Wkva, Wkvb, out_0, out_1):
         regroup(5)
         quantise(4)
         project_rope(0)
+        gather_x(1, 0, by_scalar)
+        quantise_x(1)
+        project(1)
         regroup(6)
         quantise(5)
         gather_c(0)
-        gather_x(1, 0, by_scalar)
         regroup(7)
         quantise(6)
         rope_products(0)
         quantise_c(0)
         rope_sums(0)
         expand(0, 0, 0)
-        empty(0, 0, 0)
         expand(0, 0, 1)
-        quantise_x(1)
+        gather_c(1)
         regroup(8)
         quantise(7)
+        empty(0, 0, 0)
         empty(0, 0, 1)
         expand(0, 0, 2)
-        spread_rope(0)
-        project(1)
-        quantise(8)
-        regroup(9)
-        expand(0, 0, 3)
         empty(0, 0, 2)
+        quantise(8)
+        expand(0, 0, 3)
         empty(0, 0, 3)
+        spread_rope(0)
         store(0, 0)
-        gather_c(1)
-        transpose_x(2)
+        regroup(9)
         rope_products(1)
         quantise_c(1)
+        transpose_x(2)
         rope_sums(1)
         expand(1, 0, 0)
         expand(1, 0, 1)
-        gather_x(2, 0, by_vector)
         empty(1, 0, 0)
         empty(1, 0, 1)
+        gather_x(2, 0, by_vector)
+        quantise(9)
         spread_rope(1)
-        gather_x(2, 1, by_vector)
         expand(1, 0, 2)
         expand(1, 0, 3)
         empty(1, 0, 2)
         empty(1, 0, 3)
         store(1, 0)
-        quantise(9)
         regroup(10)
+        gather_x(2, 1, by_vector)
         quantise_x(2)
+        expand(0, 1, 0)
         quantise(10)
         regroup(11)
-        expand(0, 1, 0)
-        project(2)
+        project_c(2, (0, 1))
         empty(0, 1, 0)
+        expand(0, 1, 1)
         quantise(11)
         regroup(12)
-        gather_c(2)
-        expand(0, 1, 1)
-        expand(0, 1, 2)
+        project_c(2, (2, 3))
+        project_rope(2)
         empty(0, 1, 1)
+        expand(0, 1, 2)
+        gather_c(2)
         empty(0, 1, 2)
         quantise(12)
+        expand(0, 1, 3)
+        empty(0, 1, 3)
+        store(0, 1)
         rope_products(2)
         quantise_c(2)
         rope_sums(2)
         transpose_x(3)
-        expand(0, 1, 3)
-        empty(0, 1, 3)
-        store(0, 1)
         spread_rope(2)
         expand(1, 1, 0)
         expand(1, 1, 1)

@@ -47,13 +47,13 @@ def span(index, width):
 def tile_multilatentattention_pb_kernel(tc, x, Wkva, Wkvb, out_0, out_1):
     nc = tc.nc
     x_batches = x.rearrange("b (p e) k -> b p e k", e=2)
-    kf_rows = out_0.rearrange("b (p e) h d -> b e p (h d)", e=2)
-    v_rows = out_1.rearrange("b (p e) h d -> b e p (h d)", e=2)
+    kf_rows = out_0.rearrange("b (p e) h d -> b e p h d", e=2)
+    v_rows = out_1.rearrange("b (p e) h d -> b e p h d", e=2)
 
     with ExitStack() as ctx:
         const = ctx.enter_context(tc.tile_pool(name="const", bufs=1))
         raw = ctx.enter_context(tc.tile_pool(name="raw", bufs=1))
-        stage = ctx.enter_context(tc.tile_pool(name="stage", bufs=3))
+        stage = ctx.enter_context(tc.tile_pool(name="stage", bufs=4))
         x_pool = ctx.enter_context(tc.tile_pool(name="x_pool", bufs=2))
         c_pool = ctx.enter_context(tc.tile_pool(name="c_pool", bufs=3))
         rope_pool = ctx.enter_context(tc.tile_pool(name="rope_pool", bufs=2))
@@ -293,12 +293,13 @@ def tile_multilatentattention_pb_kernel(tc, x, Wkva, Wkvb, out_0, out_1):
                 kf_tiles[i] = kf_tile
             return kf_tiles[i]
 
-        def spread_rope(i):
+        def spread_rope(i, part=slice(0, HEADS)):
             nc.vector.tensor_copy(
-                out=kf_tile_of(i)[:, :, NOPE:],
-                in_=rope_tiles[i][:].rearrange("p j e -> p (j e)").unsqueeze(1).to_broadcast([P, HEADS, ROPE]),
+                out=kf_tile_of(i)[:, part, NOPE:],
+                in_=rope_tiles[i][:].rearrange("p j e -> p (j e)").unsqueeze(1).to_broadcast([P, part.stop - part.start, ROPE]),
             )
 
+        halves = (slice(0, HEADS // 2), slice(HEADS // 2, HEADS))
         kv_banks = {}
 
         def expand(i, kind, q):
@@ -324,11 +325,9 @@ def tile_multilatentattention_pb_kernel(tc, x, Wkva, Wkvb, out_0, out_1):
                     v_tiles[i] = v_tile
                 nc.scalar.copy(out=v_tiles[i][:, span(q, HEAD_GROUP), :], in_=kv_banks[i, 1, q][:])
 
-        def store(i, kind):
-            if kind == 0:
-                nc.sync.dma_start(out=kf_rows[i // 2, i % 2], in_=kf_tiles[i][:].rearrange("p h d -> p (h d)"))
-            else:
-                nc.sync.dma_start(out=v_rows[i // 2, i % 2], in_=v_tiles[i][:].rearrange("p h d -> p (h d)"))
+        def store(i, kind, part=slice(0, HEADS)):
+            tile, rows = (kf_tiles[i], kf_rows) if kind == 0 else (v_tiles[i], v_rows)
+            nc.sync.dma_start(out=rows[i // 2, i % 2, :, part, :], in_=tile[:, part, :])
 
         by_vector, by_scalar = nc.vector.tensor_copy, nc.scalar.copy
         regroup(0)
@@ -352,9 +351,8 @@ def tile_multilatentattention_pb_kernel(tc, x, Wkva, Wkvb, out_0, out_1):
         quantise(4)
         project_rope(0)
         gather_x(1, 0, by_scalar)
-        quantise_x(1)
-        project(1)
         regroup(6)
+        quantise_x(1)
         quantise(5)
         gather_c(0)
         regroup(7)
@@ -364,76 +362,113 @@ def tile_multilatentattention_pb_kernel(tc, x, Wkva, Wkvb, out_0, out_1):
         rope_sums(0)
         expand(0, 0, 0)
         expand(0, 0, 1)
-        gather_c(1)
+        project(1)
         regroup(8)
-        quantise(7)
+        spread_rope(0, halves[0])
         empty(0, 0, 0)
         empty(0, 0, 1)
-        expand(0, 0, 2)
-        empty(0, 0, 2)
+        store(0, 0, halves[0])
+        quantise(7)
         quantise(8)
+        regroup(9)
+        expand(0, 0, 2)
+        spread_rope(0, halves[1])
+        empty(0, 0, 2)
         expand(0, 0, 3)
         empty(0, 0, 3)
-        spread_rope(0)
-        store(0, 0)
-        regroup(9)
+        store(0, 0, halves[1])
+        gather_c(1)
         rope_products(1)
         quantise_c(1)
         transpose_x(2)
         rope_sums(1)
+        regroup(10)
         expand(1, 0, 0)
         expand(1, 0, 1)
+        spread_rope(1, halves[0])
         empty(1, 0, 0)
         empty(1, 0, 1)
-        gather_x(2, 0, by_vector)
+        store(1, 0, halves[0])
         quantise(9)
-        spread_rope(1)
         expand(1, 0, 2)
         expand(1, 0, 3)
+        spread_rope(1, halves[1])
         empty(1, 0, 2)
         empty(1, 0, 3)
-        store(1, 0)
-        regroup(10)
-        gather_x(2, 1, by_vector)
-        quantise_x(2)
-        expand(0, 1, 0)
-        quantise(10)
+        store(1, 0, halves[1])
+        gather_x(2, 0, by_vector)
         regroup(11)
-        project_c(2, (0, 1))
-        empty(0, 1, 0)
+        gather_x(2, 1, by_vector)
+        quantise(10)
+        expand(0, 1, 0)
+        transpose_x(3)
         expand(0, 1, 1)
-        quantise(11)
+        quantise_x(2)
         regroup(12)
-        project_c(2, (2, 3))
-        project_rope(2)
+        empty(0, 1, 0)
         empty(0, 1, 1)
+        store(0, 1, halves[0])
+        quantise(11)
+        project_c(2, (0, 1))
         expand(0, 1, 2)
-        gather_c(2)
-        empty(0, 1, 2)
         quantise(12)
+        empty(0, 1, 2)
         expand(0, 1, 3)
         empty(0, 1, 3)
-        store(0, 1)
+        store(0, 1, halves[1])
+        gather_x(3, 0, by_vector)
+        project_c(2, (2, 3))
+        project_rope(2)
+        gather_x(3, 1, by_vector)
+        expand(1, 1, 0)
+        expand(1, 1, 1)
+        empty(1, 1, 0)
+        empty(1, 1, 1)
+        store(1, 1, halves[0])
+        gather_c(2)
+        quantise_x(3)
+        expand(1, 1, 2)
+        expand(1, 1, 3)
+        empty(1, 1, 2)
+        empty(1, 1, 3)
+        store(1, 1, halves[1])
         rope_products(2)
         quantise_c(2)
         rope_sums(2)
-        transpose_x(3)
-        spread_rope(2)
-        expand(1, 1, 0)
-        expand(1, 1, 1)
-        expand(1, 1, 2)
-        expand(1, 1, 3)
-        empty(1, 1, 0)
-        empty(1, 1, 1)
-        empty(1, 1, 2)
-        empty(1, 1, 3)
-        store(1, 1)
-        gather_x(3, 0, by_vector)
-        gather_x(3, 1, by_vector)
-        quantise_x(3)
+        spread_rope(2, halves[0])
         transpose_x(4)
+        expand(2, 0, 0)
+        expand(2, 0, 1)
+        empty(2, 0, 0)
+        empty(2, 0, 1)
+        store(2, 0, halves[0])
+        spread_rope(2, halves[1])
+        project(3)
+        expand(2, 0, 2)
+        expand(2, 0, 3)
+        empty(2, 0, 2)
+        empty(2, 0, 3)
+        store(2, 0, halves[1])
+        gather_x(4, 0, by_vector)
+        gather_c(3)
+        gather_x(4, 1, by_vector)
+        rope_products(3)
+        expand(2, 1, 0)
+        expand(2, 1, 1)
+        empty(2, 1, 0)
+        empty(2, 1, 1)
+        quantise_c(3)
+        rope_sums(3)
+        expand(2, 1, 2)
+        expand(2, 1, 3)
+        empty(2, 1, 2)
+        empty(2, 1, 3)
+        store(2, 1)
+        spread_rope(3)
+        quantise_x(4)
+        transpose_x(5)
 
-        for i in range(2, TOKEN_TILES):
+        for i in range(3, TOKEN_TILES):
             for q in range(HEAD_GROUPS):
                 expand(i, 0, q)
                 empty(i, 0, q)

@@ -34,7 +34,7 @@ HEAD_GROUPS = HEADS // HEAD_GROUP
 UNIT = BANK * PACK
 RUN = 4
 BATCHES = 4
-PIECE = 4
+PIECE = 8
 ROUND_MAGIC = 1.5 * 2.0**23
 
 FLOPS = 2 * TOKENS * D_MODEL * (LATENT + ROPE) + 2 * TOKENS * LATENT * HEADS * (NOPE + VDIM)
@@ -86,11 +86,9 @@ def tile_multilatentattention_pb_kernel(tc, x, Wkva, Wkvb, out_0, out_1):
         load_wkva(2)
         load_x(0, slice(0, 1))
         load_wkva(3)
-        load_x(0, slice(1, 2))
         load_wkvb(0)
+        load_x(0, slice(1, 2))
         load_wkvb(1)
-        load_wkvb(2)
-        load_wkvb(3)
         load_x(1, slice(0, 2))
         load_x(2, slice(0, 2))
         load_x(3, slice(0, 2))
@@ -343,34 +341,34 @@ def tile_multilatentattention_pb_kernel(tc, x, Wkva, Wkvb, out_0, out_1):
         quantise_x(0)
         quantise(2)
         regroup(4)
-        transpose_x(1)
         quantise(3)
-        gather_x(1, 1, by_scalar)
         project_c(0, (0, 1, 2, 3))
         regroup(5)
         quantise(4)
         project_rope(0)
-        gather_x(1, 0, by_scalar)
+        transpose_x(1)
         regroup(6)
-        quantise_x(1)
         quantise(5)
+        gather_x(1, 1, by_scalar)
+        gather_x(1, 0, by_scalar)
         gather_c(0)
-        regroup(7)
         quantise(6)
         rope_products(0)
         quantise_c(0)
         rope_sums(0)
+        quantise_x(1)
         expand(0, 0, 0)
         expand(0, 0, 1)
         project(1)
-        regroup(8)
         spread_rope(0, halves[0])
+        regroup(7)
+        regroup(8)
         empty(0, 0, 0)
         empty(0, 0, 1)
         store(0, 0, halves[0])
         quantise(7)
-        quantise(8)
         regroup(9)
+        quantise(8)
         expand(0, 0, 2)
         spread_rope(0, halves[1])
         empty(0, 0, 2)

@@ -34,6 +34,10 @@ HEAD_GROUPS = HEADS // HEAD_GROUP
 UNIT = BANK * PACK
 RUN = 4
 BATCHES = 4
+KIB = 1024
+WB_OFFSET = 0
+WA_OFFSET = 32 * KIB
+X_OFFSET = 52 * KIB
 PIECE = 8
 ROUND_MAGIC = 1.5 * 2.0**23
 
@@ -47,8 +51,8 @@ def span(index, width):
 def tile_multilatentattention_pb_kernel(tc, x, Wkva, Wkvb, out_0, out_1):
     nc = tc.nc
     x_batches = x.rearrange("b (p e) k -> b p e k", e=2)
-    kf_rows = out_0.rearrange("b (p e) h d -> b e p h d", e=2)
-    v_rows = out_1.rearrange("b (p e) h d -> b e p h d", e=2)
+    kf_rows = out_0.rearrange("b (p e) h d -> b p e h d", e=2)
+    v_rows = out_1.rearrange("b (p e) h d -> b p e h d", e=2)
 
     with ExitStack() as ctx:
         const = ctx.enter_context(tc.tile_pool(name="const", bufs=1))
@@ -63,9 +67,12 @@ def tile_multilatentattention_pb_kernel(tc, x, Wkva, Wkvb, out_0, out_1):
         psum_kv = ctx.enter_context(tc.psum_pool(name="psum_kv", bufs=4))
         ctx.enter_context(tc.manual_schedule())
 
-        x_raw = [raw.tile([P, 2, D_MODEL], BF16, name="x_raw%d" % b) for b in range(BATCHES)]
-        wa_raw = raw.tile([P, X_PASSES, PACK, LATENT + ROPE], BF16)
-        wb_raw = raw.tile([P, HEADS // PIECE, PACK, PIECE * (NOPE + VDIM)], BF16)
+        x_first = raw.tile([P, 2, D_MODEL], BF16, offset=X_OFFSET)
+        x_second = raw.tile([P, 2, D_MODEL], BF16, offset=X_OFFSET + 8 * KIB)
+        x_last = raw.tile([P, 2, 2, D_MODEL], BF16, offset=X_OFFSET + 16 * KIB)
+        x_raw = [x_first[:], x_second[:], x_last[:, 0], x_last[:, 1]]
+        wa_raw = raw.tile([P, X_PASSES, PACK, LATENT + ROPE], BF16, offset=WA_OFFSET)
+        wb_raw = raw.tile([P, HEADS // PIECE, PACK, PIECE * (NOPE + VDIM)], BF16, offset=WB_OFFSET)
 
         def load_wkva(g):
             nc.sync.dma_start(
@@ -90,8 +97,7 @@ def tile_multilatentattention_pb_kernel(tc, x, Wkva, Wkvb, out_0, out_1):
         load_x(0, slice(1, 2))
         load_wkvb(1)
         load_x(1, slice(0, 2))
-        load_x(2, slice(0, 2))
-        load_x(3, slice(0, 2))
+        nc.sync.dma_start(out=x_last[:], in_=x[2:4].rearrange("b (p e) k -> p b e k", e=2))
 
         ident = const.tile([P, P], F32)
         make_identity(nc, ident[:])
@@ -194,8 +200,8 @@ def tile_multilatentattention_pb_kernel(tc, x, Wkva, Wkvb, out_0, out_1):
         c_tiles = {}
         c_quantised = {}
         rope_tiles = {}
-        kf_tiles = {}
-        v_tiles = {}
+        kf_batches = {}
+        v_batches = {}
 
         def transpose_x(i):
             words = x_raw[i // 2][:, i % 2, :].bitcast(F32).rearrange("r (g p u) -> r g u p", g=X_PASSES, u=2)
@@ -286,10 +292,26 @@ def tile_multilatentattention_pb_kernel(tc, x, Wkva, Wkvb, out_0, out_1):
             rope_tiles[i] = rotated
 
         def kf_tile_of(i):
-            if i not in kf_tiles:
-                kf_tile = out_pool.tile([P, HEADS, NOPE + ROPE], F32)
-                kf_tiles[i] = kf_tile
-            return kf_tiles[i]
+            b = i // 2
+            if b not in kf_batches:
+                shape = [P, 2, HEADS, NOPE + ROPE]
+                if b == 1:
+                    kf_late = raw.tile(shape, F32, name="kf_over_wkva", offset=WA_OFFSET)
+                    kf_batches[b] = kf_late
+                elif b == 2:
+                    kf_late = raw.tile(shape, F32, name="kf_over_wkvb", offset=WB_OFFSET)
+                    kf_batches[b] = kf_late
+                else:
+                    kf_batch = out_pool.tile(shape, F32, bufs=1)
+                    kf_batches[b] = kf_batch
+            return kf_batches[b][:, i % 2]
+
+        def v_tile_of(i):
+            b = i // 2
+            if b not in v_batches:
+                v_batch = out_pool.tile([P, 2, HEADS, VDIM], F32, bufs=2)
+                v_batches[b] = v_batch
+            return v_batches[b][:, i % 2]
 
         def spread_rope(i, part=slice(0, HEADS)):
             nc.vector.tensor_copy(
@@ -318,14 +340,15 @@ def tile_multilatentattention_pb_kernel(tc, x, Wkva, Wkvb, out_0, out_1):
             if kind == 0:
                 nc.scalar.copy(out=kf_tile_of(i)[:, span(q, HEAD_GROUP), :NOPE], in_=kv_banks[i, 0, q][:])
             else:
-                if q == 0:
-                    v_tile = out_pool.tile([P, HEADS, VDIM], F32)
-                    v_tiles[i] = v_tile
-                nc.scalar.copy(out=v_tiles[i][:, span(q, HEAD_GROUP), :], in_=kv_banks[i, 1, q][:])
+                nc.scalar.copy(out=v_tile_of(i)[:, span(q, HEAD_GROUP), :], in_=kv_banks[i, 1, q][:])
 
         def store(i, kind, part=slice(0, HEADS)):
-            tile, rows = (kf_tiles[i], kf_rows) if kind == 0 else (v_tiles[i], v_rows)
-            nc.sync.dma_start(out=rows[i // 2, i % 2, :, part, :], in_=tile[:, part, :])
+            tile, rows = (kf_tile_of(i), kf_rows) if kind == 0 else (v_tile_of(i), v_rows)
+            nc.sync.dma_start(out=rows[i // 2, :, i % 2, part, :], in_=tile[:, part, :])
+
+        def store_batch(b, kind):
+            tile, rows = (kf_batches[b], kf_rows) if kind == 0 else (v_batches[b], v_rows)
+            nc.sync.dma_start(out=rows[b], in_=tile[:])
 
         by_vector, by_scalar = nc.vector.tensor_copy, nc.scalar.copy
         regroup(0)
@@ -474,7 +497,10 @@ def tile_multilatentattention_pb_kernel(tc, x, Wkva, Wkvb, out_0, out_1):
                     gather_x(i + 2, q, by_vector)
                 if i + 1 < TOKEN_TILES and q == 1:
                     project_c(i + 1, (0, 1))
-            store(i, 0)
+            if i < 6:
+                store(i, 0)
+            elif i == 7:
+                store_batch(3, 0)
             if i + 1 < TOKEN_TILES:
                 project_c(i + 1, (2, 3))
                 project_rope(i + 1)
@@ -488,7 +514,10 @@ def tile_multilatentattention_pb_kernel(tc, x, Wkva, Wkvb, out_0, out_1):
             for q in range(HEAD_GROUPS):
                 expand(i, 1, q)
                 empty(i, 1, q)
-            store(i, 1)
+            if i == 3:
+                store(i, 1)
+            elif i % 2 == 1:
+                store_batch(i // 2, 1)
             if i + 1 < TOKEN_TILES:
                 spread_rope(i + 1)
             if i + 3 < TOKEN_TILES:

@@ -186,8 +186,7 @@ def tile_multilatentattention_pb_kernel(tc, x, Wkva, Wkvb, out_0, out_1):
                 target = grouped[:].rearrange("p (n c i j) -> p n c j i", n=4, i=RUN, j=PACK)
                 source = units[n][0].rearrange("p n (c i) j -> p n c j i", i=RUN)
                 nc.vector.tensor_copy(out=target[:, :2], in_=source[:, :2])
-                for block in range(2, 4):
-                    nc.scalar.copy(out=target[:, block], in_=source[:, block])
+                nc.scalar.copy(out=target[:, 2:], in_=source[:, 2:])
 
         def quantise(n):
             nc.vector.quantize_mx(out=units[n][1].bitcast(FP8X4), scales=units[n][2], in_=unit_tiles[n][:])
@@ -384,14 +383,15 @@ def tile_multilatentattention_pb_kernel(tc, x, Wkva, Wkvb, out_0, out_1):
         expand(0, 0, 1)
         project(1)
         spread_rope(0, halves[0])
+        regroup(9)
         regroup(7)
         regroup(8)
         empty(0, 0, 0)
         empty(0, 0, 1)
         store(0, 0, halves[0])
         quantise(7)
-        regroup(9)
         quantise(8)
+        quantise(9)
         expand(0, 0, 2)
         spread_rope(0, halves[1])
         empty(0, 0, 2)
@@ -410,7 +410,6 @@ def tile_multilatentattention_pb_kernel(tc, x, Wkva, Wkvb, out_0, out_1):
         empty(1, 0, 0)
         empty(1, 0, 1)
         store(1, 0, halves[0])
-        quantise(9)
         expand(1, 0, 2)
         expand(1, 0, 3)
         spread_rope(1, halves[1])

@@ -97,7 +97,6 @@ def tile_multilatentattention_pb_kernel(tc, x, Wkva, Wkvb, out_0, out_1):
         load_x(0, slice(1, 2))
         load_wkvb(1)
         load_x(1, slice(0, 2))
-        nc.sync.dma_start(out=x_last[:], in_=x[2:4].rearrange("b (p e) k -> p b e k", e=2))
 
         ident = const.tile([P, P], F32)
         make_identity(nc, ident[:])
@@ -385,6 +384,7 @@ def tile_multilatentattention_pb_kernel(tc, x, Wkva, Wkvb, out_0, out_1):
         spread_rope(0, halves[0])
         regroup(9)
         regroup(7)
+        nc.scalar.dma_start(out=x_last[:], in_=x[2:4].rearrange("b (p e) k -> p b e k", e=2))
         regroup(8)
         empty(0, 0, 0)
         empty(0, 0, 1)

import math
from contextlib import ExitStack

import concourse.mybir as mybir
from concourse.masks import make_identity

BF16 = mybir.dt.bfloat16
F32 = mybir.dt.float32
U32 = mybir.dt.uint32
U8 = mybir.dt.uint8
FP8X4 = mybir.dt.float8_e4m3fn_x4
ALU = mybir.AluOpType

P = 128
PACK = 4
K_PASS = P * PACK
BANK = 512

TOKENS = 4 * 256
POSITIONS = 256
D_MODEL = 2048
HEADS = 16
LATENT = 512
ROPE = 128
NOPE = 128
VDIM = 128
ROPE_BASE = 10000.0

TOKEN_TILES = TOKENS // P
X_PASSES = D_MODEL // K_PASS
PAIRS = ROPE // 2
HEAD_GROUP = BANK // NOPE
HEAD_GROUPS = HEADS // HEAD_GROUP
UNIT = BANK * PACK
RUN = 4
BATCHES = 4
KIB = 1024
WB_OFFSET = 0
WA_OFFSET = 32 * KIB
X_OFFSET = 52 * KIB
PIECE = 8
ROUND_MAGIC = 1.5 * 2.0**23

FLOPS = 2 * TOKENS * D_MODEL * (LATENT + ROPE) + 2 * TOKENS * LATENT * HEADS * (NOPE + VDIM)


def span(index, width):
    return slice(index * width, (index + 1) * width)


def tile_multilatentattention_pb_kernel(tc, x, Wkva, Wkvb, out_0, out_1):
    nc = tc.nc
    x_batches = x.rearrange("b (p e) k -> b p e k", e=2)
    kf_rows = out_0.rearrange("b (p e) h d -> b p e h d", e=2)
    v_rows = out_1.rearrange("b (p e) h d -> b p e h d", e=2)

    with ExitStack() as ctx:
        const = ctx.enter_context(tc.tile_pool(name="const", bufs=1))
        raw = ctx.enter_context(tc.tile_pool(name="raw", bufs=1))
        stage = ctx.enter_context(tc.tile_pool(name="stage", bufs=4))
        x_pool = ctx.enter_context(tc.tile_pool(name="x_pool", bufs=2))
        c_pool = ctx.enter_context(tc.tile_pool(name="c_pool", bufs=3))
        rope_pool = ctx.enter_context(tc.tile_pool(name="rope_pool", bufs=2))
        out_pool = ctx.enter_context(tc.tile_pool(name="out_pool", bufs=3))
        psum_x = ctx.enter_context(tc.psum_pool(name="psum_x", bufs=2))
        psum_c = ctx.enter_context(tc.psum_pool(name="psum_c", bufs=1))
        psum_kv = ctx.enter_context(tc.psum_pool(name="psum_kv", bufs=4))
        ctx.enter_context(tc.manual_schedule())

        x_first = raw.tile([P, 2, D_MODEL], BF16, offset=X_OFFSET)
        x_second = raw.tile([P, 2, D_MODEL], BF16, offset=X_OFFSET + 8 * KIB)
        x_last = raw.tile([P, 2, 2, D_MODEL], BF16, offset=X_OFFSET + 16 * KIB)
        x_raw = [x_first[:], x_second[:], x_last[:, 0], x_last[:, 1]]
        wa_raw = raw.tile([P, X_PASSES, PACK, LATENT + ROPE], BF16, offset=WA_OFFSET)
        wb_raw = raw.tile([P, HEADS // PIECE, PACK, PIECE * (NOPE + VDIM)], BF16, offset=WB_OFFSET)

        def load_wkva(g):
            nc.sync.dma_start(
                out=wa_raw[:, g, :, :], in_=Wkva[span(g, K_PASS), :].rearrange("(p j) c -> p j c", j=PACK)
            )

        wb_by_partition = Wkvb.rearrange("(p t) n -> p t n", t=PACK)
        def load_wkvb(piece):
            nc.sync.dma_start(
                out=wb_raw[:, piece, :, :], in_=wb_by_partition[:, :, span(piece, PIECE * (NOPE + VDIM))]
            )

        def load_x(b, parities):
            nc.sync.dma_start(out=x_raw[b][:, parities, :], in_=x_batches[b, :, parities, :])

        load_wkva(0)
        load_wkva(1)
        load_wkva(2)
        load_x(0, slice(0, 1))
        load_wkva(3)
        load_wkvb(0)
        load_x(0, slice(1, 2))
        load_wkvb(1)
        load_x(1, slice(0, 2))

        ident = const.tile([P, P], F32)
        make_identity(nc, ident[:])
        first_sin = const.tile([P, 2], F32)
        nc.vector.memset(first_sin[:, 0:1], 0.0)
        nc.scalar.activation(
            out=first_sin[:, 1:2], in_=first_sin[:, 0:1], func=mybir.ActivationFunctionType.Sin
        )

        freq = const.tile([P, PAIRS], F32)
        nc.vector.memset(freq[:, 0:1], 1.0)
        for doubling in range(6):
            w = 2**doubling
            nc.vector.tensor_scalar(
                out=freq[:, w : 2 * w],
                in0=freq[:, 0:w],
                scalar1=ROPE_BASE ** (-2.0 * w / ROPE),
                scalar2=None,
                op0=ALU.mult,
            )
        position = const.tile([P, 2], F32)
        nc.gpsimd.iota(
            position[:], pattern=[[1, 2]], base=0, channel_multiplier=2, allow_small_or_imprecise_dtypes=True
        )
        turns = const.tile([P, 2 * 2 * PAIRS], F32)
        turns_view = turns[:].rearrange("p (f h j) -> p f h j", f=2, h=2)
        for parity in range(2):
            nc.vector.tensor_scalar(
                out=turns_view[:, 0, parity, :],
                in0=freq[:],
                scalar1=position[:, parity : parity + 1],
                scalar2=1.0 / (2.0 * math.pi),
                op0=ALU.mult,
                op1=ALU.mult,
            )
        nc.vector.tensor_scalar(
            out=turns[:, 2 * PAIRS :], in0=turns[:, : 2 * PAIRS], scalar1=0.25, scalar2=None, op0=ALU.add
        )
        whole_turns = const.tile([P, 2 * 2 * PAIRS], F32)
        nc.vector.tensor_scalar(
            out=whole_turns[:],
            in0=turns[:],
            scalar1=ROUND_MAGIC,
            scalar2=ROUND_MAGIC,
            op0=ALU.add,
            op1=ALU.subtract,
        )
        part_turns = const.tile([P, 2 * 2 * PAIRS], F32)
        nc.vector.tensor_tensor(out=part_turns[:], in0=turns[:], in1=whole_turns[:], op=ALU.subtract)
        trig = const.tile([P, 2 * 2 * PAIRS], F32)
        trig_view = trig[:].rearrange("p (f h j) -> p f h j", f=2, h=2)

        def take_sines():
            nc.scalar.activation(
                out=trig[:], in_=part_turns[:], func=mybir.ActivationFunctionType.Sin, scale=2.0 * math.pi
            )

        wa_codes = const.tile([P, X_PASSES * LATENT], U32, align_bytes=64)
        wa_scales = const.tile([P, X_PASSES * LATENT], U8, align_bytes=64)
        wr_codes = const.tile([P, X_PASSES * ROPE], U32, align_bytes=64)
        wr_scales = const.tile([P, X_PASSES * ROPE], U8, align_bytes=64)
        wb_codes = const.tile([P, 2 * HEADS * NOPE], U32, align_bytes=64)
        wb_scales = const.tile([P, 2 * HEADS * NOPE], U8, align_bytes=64)

        units = []
        for g in range(X_PASSES):
            units.append((None, wa_codes[:, span(g, LATENT)], wa_scales[:, span(g, LATENT)]))
        units.append((wa_raw[:, :, :, LATENT:].rearrange("p g j c -> p g c j"), wr_codes[:], wr_scales[:]))
        for kind in range(2):
            for q in range(HEAD_GROUPS):
                in_piece = q % (PIECE // HEAD_GROUP)
                heads = wb_raw[:, q * HEAD_GROUP // PIECE, :, :].rearrange("p t (h k c) -> p k h c t", k=2, c=NOPE)
                columns = span(kind * HEAD_GROUPS + q, BANK)
                units.append((heads[:, kind, span(in_piece, HEAD_GROUP)], wb_codes[:, columns], wb_scales[:, columns]))
        unit_tiles = {}

        def regroup(n):
            grouped = stage.tile([P, UNIT], BF16, align_bytes=64)
            unit_tiles[n] = grouped
            if n < X_PASSES:
                target = grouped[:].rearrange("p (t m j) -> p t m j", t=PACK, j=PACK)
                source = wa_raw[:, n, :, :LATENT].rearrange("p j (m t) -> p t m j", t=PACK)
                nc.vector.tensor_copy(out=target[:, :2], in_=source[:, :2])
                nc.scalar.copy(out=target[:, 2:], in_=source[:, 2:])
            else:
                target = grouped[:].rearrange("p (n c i j) -> p n c j i", n=4, i=RUN, j=PACK)
                source = units[n][0].rearrange("p n (c i) j -> p n c j i", i=RUN)
                nc.vector.tensor_copy(out=target[:, :2], in_=source[:, :2])
                nc.scalar.copy(out=target[:, 2:], in_=source[:, 2:])

        def quantise(n):
            nc.vector.quantize_mx(out=units[n][1].bitcast(FP8X4), scales=units[n][2], in_=unit_tiles[n][:])

        x_banks = {}
        x_tiles = {}
        x_quantised = {}
        c_banks = {}
        k_pe_banks = {}
        c_tiles = {}
        c_quantised = {}
        rope_tiles = {}
        kf_batches = {}
        v_batches = {}

        def transpose_x(i):
            words = x_raw[i // 2][:, i % 2, :].bitcast(F32).rearrange("r (g p u) -> r g u p", g=X_PASSES, u=2)
            for bank in range(2):
                x_t = psum_x.tile([P, 2, 2, P], F32)
                for g in range(2):
                    for u in range(2):
                        nc.tensor.transpose(out=x_t[:, g, u, :], in_=words[:, 2 * bank + g, u, :], identity=ident[:])
                x_banks[i, bank] = x_t
            x_grouped = x_pool.tile([P, D_MODEL], BF16, align_bytes=64)
            x_tiles[i] = x_grouped

        def gather_x(i, bank, copy):
            words = x_tiles[i][:].bitcast(F32).rearrange("p (g r u) -> p g r u", g=X_PASSES, u=2)
            copy(out=words[:, span(bank, 2), :, :], in_=x_banks[i, bank][:].rearrange("p g u r -> p g r u"))

        def quantise_x(i):
            x_codes = x_pool.tile([P, X_PASSES * P], U32, align_bytes=64)
            x_scales = x_pool.tile([P, X_PASSES * P], U8, align_bytes=64)
            nc.vector.quantize_mx(out=x_codes[:].bitcast(FP8X4), scales=x_scales[:], in_=x_tiles[i][:])
            x_quantised[i] = (x_codes, x_scales)

        def project_c(i, pieces):
            x_codes, x_scales = x_quantised[i]
            if pieces[0] == 0:
                c_t = psum_c.tile([P, PACK, P], F32)
                c_banks[i] = c_t
            c_t = c_banks[i]
            for t in pieces:
                for g in range(X_PASSES):
                    nc.tensor.matmul_mx(
                        out=c_t[:, t, :],
                        lhsT=wa_codes[:, span(g * PACK + t, P)].bitcast(FP8X4),
                        lhsT_scale=wa_scales[:, span(g * PACK + t, P)],
                        rhs=x_codes[:, span(g, P)].bitcast(FP8X4),
                        rhs_scale=x_scales[:, span(g, P)],
                        start=(g == 0),
                        stop=(g == X_PASSES - 1),
                    )

        def project_rope(i):
            x_codes, x_scales = x_quantised[i]
            k_pe = psum_c.tile([P, ROPE], F32)
            for g in range(X_PASSES):
                nc.tensor.matmul_mx(
                    out=k_pe[:],
                    lhsT=x_codes[:, span(g, P)].bitcast(FP8X4),
                    lhsT_scale=x_scales[:, span(g, P)],
                    rhs=wr_codes[:, span(g, ROPE)].bitcast(FP8X4),
                    rhs_scale=wr_scales[:, span(g, ROPE)],
                    start=(g == 0),
                    stop=(g == X_PASSES - 1),
                )
            k_pe_banks[i] = k_pe

        def project(i):
            project_c(i, (0, 1, 2, 3))
            project_rope(i)

        def gather_c(i):
            c_grouped = c_pool.tile([P, P, PACK], BF16, align_bytes=64)
            nc.vector.tensor_copy(out=c_grouped[:], in_=c_banks[i][:].rearrange("p t r -> p r t"))
            c_tiles[i] = c_grouped

        def quantise_c(i):
            c_codes = c_pool.tile([P, P], U32, align_bytes=64)
            c_scales = c_pool.tile([P, P], U8, align_bytes=64)
            nc.vector.quantize_mx(
                out=c_codes[:].bitcast(FP8X4), scales=c_scales[:], in_=c_tiles[i][:].rearrange("p r t -> p (r t)")
            )
            c_quantised[i] = (c_codes, c_scales)

        def rope_products(i):
            sin = trig_view[:, 0, i % 2, :].unsqueeze(2).to_broadcast([P, PAIRS, 2])
            cos = trig_view[:, 1, i % 2, :].unsqueeze(2).to_broadcast([P, PAIRS, 2])
            pairs = k_pe_banks[i][:].rearrange("p (j e) -> p j e", e=2)
            by_cos = rope_pool.tile([P, PAIRS, 2], F32)
            by_sin = rope_pool.tile([P, PAIRS, 2], F32)
            nc.vector.tensor_tensor(out=by_cos[:], in0=pairs, in1=cos, op=ALU.mult)
            nc.vector.tensor_tensor(out=by_sin[:], in0=pairs, in1=sin, op=ALU.mult)
            rope_tiles[i] = (by_cos, by_sin)

        def rope_sums(i):
            by_cos, by_sin = rope_tiles[i]
            rotated = rope_pool.tile([P, PAIRS, 2], F32)
            nc.vector.tensor_tensor(out=rotated[:, :, 0], in0=by_cos[:, :, 0], in1=by_sin[:, :, 1], op=ALU.subtract)
            nc.vector.tensor_tensor(out=rotated[:, :, 1], in0=by_sin[:, :, 0], in1=by_cos[:, :, 1], op=ALU.add)
            rope_tiles[i] = rotated

        def kf_tile_of(i):
            b = i // 2
            if b not in kf_batches:
                shape = [P, 2, HEADS, NOPE + ROPE]
                if b == 1:
                    kf_late = raw.tile(shape, F32, name="kf_over_wkva", offset=WA_OFFSET)
                    kf_batches[b] = kf_late
                elif b == 2:
                    kf_late = raw.tile(shape, F32, name="kf_over_wkvb", offset=WB_OFFSET)
                    kf_batches[b] = kf_late
                else:
                    kf_batch = out_pool.tile(shape, F32, bufs=1)
                    kf_batches[b] = kf_batch
            return kf_batches[b][:, i % 2]

        def v_tile_of(i):
            b = i // 2
            if b not in v_batches:
                v_batch = out_pool.tile([P, 2, HEADS, VDIM], F32, bufs=2)
                v_batches[b] = v_batch
            return v_batches[b][:, i % 2]

        def spread_rope(i, part=slice(0, HEADS)):
            nc.vector.tensor_copy(
                out=kf_tile_of(i)[:, part, NOPE:],
                in_=rope_tiles[i][:].rearrange("p j e -> p (j e)").unsqueeze(1).to_broadcast([P, part.stop - part.start, ROPE]),
            )

        halves = (slice(0, HEADS // 2), slice(HEADS // 2, HEADS))
        kv_banks = {}

        def expand(i, kind, q):
            c_codes, c_scales = c_quantised[i]
            kv = psum_kv.tile([P, HEAD_GROUP, NOPE], F32)
            nc.tensor.matmul_mx(
                out=kv[:].rearrange("p h c -> p (h c)"),
                lhsT=c_codes[:].bitcast(FP8X4),
                lhsT_scale=c_scales[:],
                rhs=wb_codes[:, span(kind * HEAD_GROUPS + q, BANK)].bitcast(FP8X4),
                rhs_scale=wb_scales[:, span(kind * HEAD_GROUPS + q, BANK)],
                start=True,
                stop=True,
            )
            kv_banks[i, kind, q] = kv

        def empty(i, kind, q):
            if kind == 0:
                nc.scalar.copy(out=kf_tile_of(i)[:, span(q, HEAD_GROUP), :NOPE], in_=kv_banks[i, 0, q][:])
            else:
                nc.scalar.copy(out=v_tile_of(i)[:, span(q, HEAD_GROUP), :], in_=kv_banks[i, 1, q][:])

        def store(i, kind, part=slice(0, HEADS)):
            tile, rows = (kf_tile_of(i), kf_rows) if kind == 0 else (v_tile_of(i), v_rows)
            nc.sync.dma_start(out=rows[i // 2, :, i % 2, part, :], in_=tile[:, part, :])

        def store_batch(b, kind):
            tile, rows = (kf_batches[b], kf_rows) if kind == 0 else (v_batches[b], v_rows)
            nc.sync.dma_start(out=rows[b], in_=tile[:])

        by_vector, by_scalar = nc.vector.tensor_copy, nc.scalar.copy
        regroup(0)
        regroup(1)
        transpose_x(0)
        quantise(0)
        take_sines()
        regroup(2)
        quantise(1)
        gather_x(0, 0, by_vector)
        gather_x(0, 1, by_scalar)
        regroup(3)
        quantise_x(0)
        quantise(2)
        regroup(4)
        quantise(3)
        project_c(0, (0, 1, 2, 3))
        regroup(5)
        quantise(4)
        project_rope(0)
        transpose_x(1)
        regroup(6)
        quantise(5)
        gather_x(1, 1, by_scalar)
        gather_x(1, 0, by_scalar)
        gather_c(0)
        quantise(6)
        rope_products(0)
        quantise_c(0)
        rope_sums(0)
        quantise_x(1)
        expand(0, 0, 0)
        expand(0, 0, 1)
        project(1)
        spread_rope(0, halves[0])
        regroup(9)
        regroup(7)
        nc.scalar.dma_start(out=x_last[:], in_=x[2:4].rearrange("b (p e) k -> p b e k", e=2))
        regroup(8)
        empty(0, 0, 0)
        empty(0, 0, 1)
        store(0, 0, halves[0])
        quantise(7)
        quantise(8)
        quantise(9)
        expand(0, 0, 2)
        spread_rope(0, halves[1])
        empty(0, 0, 2)
        expand(0, 0, 3)
        empty(0, 0, 3)
        store(0, 0, halves[1])
        gather_c(1)
        rope_products(1)
        quantise_c(1)
        transpose_x(2)
        rope_sums(1)
        regroup(10)
        expand(1, 0, 0)
        expand(1, 0, 1)
        spread_rope(1, halves[0])
        empty(1, 0, 0)
        empty(1, 0, 1)
        store(1, 0, halves[0])
        expand(1, 0, 2)
        expand(1, 0, 3)
        spread_rope(1, halves[1])
        empty(1, 0, 2)
        empty(1, 0, 3)
        store(1, 0, halves[1])
        gather_x(2, 0, by_vector)
        regroup(11)
        gather_x(2, 1, by_vector)
        quantise(10)
        expand(0, 1, 0)
        transpose_x(3)
        expand(0, 1, 1)
        quantise_x(2)
        regroup(12)
        empty(0, 1, 0)
        empty(0, 1, 1)
        store(0, 1, halves[0])
        quantise(11)
        project_c(2, (0, 1))
        expand(0, 1, 2)
        quantise(12)
        empty(0, 1, 2)
        expand(0, 1, 3)
        empty(0, 1, 3)
        store(0, 1, halves[1])
        gather_x(3, 0, by_vector)
        project_c(2, (2, 3))
        project_rope(2)
        gather_x(3, 1, by_vector)
        expand(1, 1, 0)
        expand(1, 1, 1)
        empty(1, 1, 0)
        empty(1, 1, 1)
        store(1, 1, halves[0])
        gather_c(2)
        quantise_x(3)
        expand(1, 1, 2)
        expand(1, 1, 3)
        empty(1, 1, 2)
        empty(1, 1, 3)
        store(1, 1, halves[1])
        rope_products(2)
        quantise_c(2)
        rope_sums(2)
        spread_rope(2, halves[0])
        transpose_x(4)
        expand(2, 0, 0)
        expand(2, 0, 1)
        empty(2, 0, 0)
        empty(2, 0, 1)
        store(2, 0, halves[0])
        spread_rope(2, halves[1])
        project(3)
        expand(2, 0, 2)
        expand(2, 0, 3)
        empty(2, 0, 2)
        empty(2, 0, 3)
        store(2, 0, halves[1])
        gather_x(4, 0, by_vector)
        gather_c(3)
        gather_x(4, 1, by_vector)
        rope_products(3)
        expand(2, 1, 0)
        expand(2, 1, 1)
        empty(2, 1, 0)
        empty(2, 1, 1)
        quantise_c(3)
        rope_sums(3)
        expand(2, 1, 2)
        expand(2, 1, 3)
        empty(2, 1, 2)
        empty(2, 1, 3)
        store(2, 1)
        spread_rope(3)
        quantise_x(4)
        transpose_x(5)

        for i in range(3, TOKEN_TILES):
            for q in range(HEAD_GROUPS):
                expand(i, 0, q)
                empty(i, 0, q)
                if i + 2 < TOKEN_TILES and q < 2:
                    gather_x(i + 2, q, by_vector)
                if i + 1 < TOKEN_TILES and q == 1:
                    project_c(i + 1, (0, 1))
            if i < 6:
                store(i, 0)
            elif i == 7:
                store_batch(3, 0)
            if i + 1 < TOKEN_TILES:
                project_c(i + 1, (2, 3))
                project_rope(i + 1)
                gather_c(i + 1)
                rope_products(i + 1)
            if i + 2 < TOKEN_TILES:
                quantise_x(i + 2)
            if i + 1 < TOKEN_TILES:
                quantise_c(i + 1)
                rope_sums(i + 1)
            for q in range(HEAD_GROUPS):
                expand(i, 1, q)
                empty(i, 1, q)
            if i == 3:
                store(i, 1)
            elif i % 2 == 1:
                store_batch(i // 2, 1)
            if i + 1 < TOKEN_TILES:
                spread_rope(i + 1)
            if i + 3 < TOKEN_TILES:
                transpose_x(i + 3)
